import numpy as np
import ml_dtypes

BF16 = ml_dtypes.bfloat16


def bf(x):
    return np.asarray(x, np.float32).astype(BF16)


def f32(x):
    return np.asarray(x, np.float32)


def f64(x):
    return np.asarray(x).astype(np.float64)


def striped(idx):
    return np.tile(idx.reshape(-1, 16).T, (8, 1))


C, S, N, E, R, NG = 256, 2048, 512, 8, 16, 2
K = E * R
OD = N // NG
SCALING = 16.0 / 8.0


def setup_inputs():
    return {"base": f32(np.random.standard_normal((C, S))), "h": f32(np.random.standard_normal((C, NG * K))), "logits": f32(np.random.standard_normal((C, E))), "bw": bf(0.25 * np.random.standard_normal((K, N))), "offs": striped(np.random.permutation(S)[:N])}


def reference(base, h, logits, bw, offs):
    idx = offs[:16].T.reshape(-1)
    p = np.exp(f64(logits))
    q = SCALING / p.sum(axis=1, keepdims=True)
    wh = (f64(h).reshape(C, NG, E, R) * p[:, None, :, None]).reshape(C, NG, K)
    u = np.einsum("cak,kao->cao", wh, f64(bw).reshape(K, NG, OD)).reshape(C, N)
    res = f64(base).copy()
    res[:, idx] = u * q
    return res

@@ -1,0 +1,89 @@
+import concourse.mybir as mybir
+from concourse.masks import make_identity
+
+F32, BF16, U16 = mybir.dt.float32, mybir.dt.bfloat16, mybir.dt.uint16
+MULT = mybir.AluOpType.mult
+MAX = mybir.AluOpType.max
+EXP = mybir.ActivationFunctionType.Exp
+COPY = mybir.ActivationFunctionType.Copy
+X = mybir.AxisListType.X
+
+P = 128
+C, S, N = 256, 2048, 512
+E, R, NG = 8, 16, 2
+K = E * R
+OD = N // NG
+BLOCKS = C // P
+
+FLOPS = 2 * C * N * K
+BYTES = 4 * C * (S - N) + 4 * C * NG * K + 4 * C * E + 2 * K * N + 2 * P * (N // 16) + 4 * C * S
+
+
+def tile_moelora_s_kernel(tc, base, h, logits, bw, offs, out):
+    nc = tc.nc
+    with (
+        tc.tile_pool(name="held", bufs=1) as held,
+        tc.tile_pool(name="work", bufs=BLOCKS) as work,
+        tc.psum_pool(name="psum", bufs=BLOCKS) as psum,
+    ):
+        offsets = held.tile([P, N // 16], U16, name="offsets")
+        nc.sync.dma_start(offsets[:], offs)
+        weights = held.tile([K, N], BF16, name="weights")
+        nc.scalar.dma_start(weights[:], bw)
+        identity = held.tile([P, P], BF16, name="identity")
+        make_identity(nc, identity[:])
+
+        router, feats, windows = [], [], []
+        for b in range(BLOCKS):
+            rows = slice(b * P, (b + 1) * P)
+            lg = work.tile([P, E], F32, name="lg")
+            nc.sync.dma_start(lg[:], logits[rows, :])
+            hb = work.tile([P, NG * K], F32, name="hb")
+            nc.scalar.dma_start(hb[:], h[rows, :])
+            router.append(lg)
+            feats.append(hb)
+        for b in range(BLOCKS):
+            rows = slice(b * P, (b + 1) * P)
+            window = work.tile([P, S], F32, name="window")
+            nc.sync.dma_start(window[:, : S // 2], base[rows, : S // 2])
+            nc.scalar.dma_start(window[:, S // 2 :], base[rows, S // 2 :])
+            windows.append(window)
+
+        for b in range(BLOCKS):
+            rows = slice(b * P, (b + 1) * P)
+            negmax = work.tile([P, 1], F32, name="negmax")
+            nc.vector.tensor_reduce(negmax[:], router[b][:], X, MAX, negate=True)
+            p = work.tile([P, E], F32, name="p")
+            psumrow = work.tile([P, 1], F32, name="psumrow")
+            nc.scalar.activation(p[:], router[b][:], EXP, bias=negmax[:], scale=1.0, accum_out=psumrow[:])
+            wh = work.tile([P, NG * K], BF16, name="wh")
+            nc.vector.tensor_tensor(
+                wh[:].rearrange("c (a e r) -> c a e r", a=NG, e=E),
+                feats[b][:].rearrange("c (a e r) -> c a e r", a=NG, e=E),
+                p[:].unsqueeze(1).unsqueeze(3).to_broadcast([P, NG, E, R]),
+                MULT,
+            )
+            half = work.tile([P, 1], F32, name="half")
+            nc.vector.tensor_scalar_mul(half[:], psumrow[:], 0.5)
+            q = work.tile([P, 1], F32, name="q")
+            nc.vector.reciprocal(q[:], half[:])
+            q_spread = work.tile([P, N], F32, name="q_spread")
+            nc.gpsimd.tensor_copy(q_spread[:], q[:].to_broadcast([P, N]))
+            flipped_ps = psum.tile([K, NG * P], BF16, name="flipped_ps")
+            for a in range(NG):
+                nc.tensor.transpose(flipped_ps[:, a * P : (a + 1) * P], wh[:, a * K : (a + 1) * K], identity[:])
+            flipped = work.tile([K, NG * P], BF16, name="flipped")
+            nc.scalar.activation(flipped[:], flipped_ps[:], COPY)
+            u = psum.tile([P, N], F32, name="u")
+            for a in range(NG):
+                nc.tensor.matmul(
+                    u[:, a * OD : (a + 1) * OD],
+                    flipped[:, a * P : (a + 1) * P],
+                    weights[:, a * OD : (a + 1) * OD],
+                    start=True,
+                    stop=True,
+                )
+            u_sb = work.tile([P, N], F32, name="u_sb")
+            nc.scalar.activation(u_sb[:], u[:], COPY)
+            nc.vector.tensor_tensor(windows[b][:].indirect(offsets[:]), u_sb[:], q_spread[:], MULT)
+            nc.sync.dma_start(out[rows, :], windows[b][:])

@@ -49,6 +49,11 @@ def tile_moelora_s_kernel(tc, base, h, logits, bw, offs, out):
             nc.scalar.dma_start(window[:, S // 2 :], base[rows, S // 2 :])
             windows.append(window)
 
+        scratch = held.tile([P, 1], F32, name="scratch")
+        nc.vector.memset(scratch[:], 0.0)
+        warmed = held.tile([P, 1], F32, name="warmed")
+        nc.scalar.activation(warmed[:], scratch[:], EXP)
+
         for b in range(BLOCKS):
             rows = slice(b * P, (b + 1) * P)
             negmax = work.tile([P, 1], F32, name="negmax")

@@ -26,22 +26,15 @@ def tile_moelora_s_kernel(tc, base, h, logits, bw, offs, out):
         tc.tile_pool(name="work", bufs=BLOCKS) as work,
         tc.psum_pool(name="psum", bufs=BLOCKS) as psum,
     ):
+        lg = held.tile([P, BLOCKS, E], F32, name="lg")
+        nc.sync.dma_start(lg[:], logits.rearrange("(b c) e -> c b e", c=P))
+        hb = held.tile([P, BLOCKS, NG * K], F32, name="hb")
+        nc.scalar.dma_start(hb[:], h.rearrange("(b c) i -> c b i", c=P))
         offsets = held.tile([P, N // 16], U16, name="offsets")
         nc.sync.dma_start(offsets[:], offs)
         weights = held.tile([K, N], BF16, name="weights")
         nc.scalar.dma_start(weights[:], bw)
-        identity = held.tile([P, P], BF16, name="identity")
-        make_identity(nc, identity[:])
-
-        router, feats, windows = [], [], []
-        for b in range(BLOCKS):
-            rows = slice(b * P, (b + 1) * P)
-            lg = work.tile([P, E], F32, name="lg")
-            nc.sync.dma_start(lg[:], logits[rows, :])
-            hb = work.tile([P, NG * K], F32, name="hb")
-            nc.scalar.dma_start(hb[:], h[rows, :])
-            router.append(lg)
-            feats.append(hb)
+        windows = []
         for b in range(BLOCKS):
             rows = slice(b * P, (b + 1) * P)
             window = work.tile([P, S], F32, name="window")
@@ -49,46 +42,64 @@ def tile_moelora_s_kernel(tc, base, h, logits, bw, offs, out):
             nc.scalar.dma_start(window[:, S // 2 :], base[rows, S // 2 :])
             windows.append(window)
 
+        identity = held.tile([P, P], BF16, name="identity")
+        make_identity(nc, identity[:])
         scratch = held.tile([P, 1], F32, name="scratch")
         nc.vector.memset(scratch[:], 0.0)
         warmed = held.tile([P, 1], F32, name="warmed")
         nc.scalar.activation(warmed[:], scratch[:], EXP)
 
+        negmax = held.tile([P, BLOCKS], F32, name="negmax")
+        nc.vector.tensor_reduce(negmax[:], lg[:], X, MAX, negate=True)
+        p = held.tile([P, BLOCKS, E], F32, name="p")
+        total = held.tile([P, BLOCKS], F32, name="total")
         for b in range(BLOCKS):
-            rows = slice(b * P, (b + 1) * P)
-            negmax = work.tile([P, 1], F32, name="negmax")
-            nc.vector.tensor_reduce(negmax[:], router[b][:], X, MAX, negate=True)
-            p = work.tile([P, E], F32, name="p")
-            psumrow = work.tile([P, 1], F32, name="psumrow")
-            nc.scalar.activation(p[:], router[b][:], EXP, bias=negmax[:], scale=1.0, accum_out=psumrow[:])
+            nc.scalar.activation(
+                p[:, b, :], lg[:, b, :], EXP, bias=negmax[:, b : b + 1], scale=1.0, accum_out=total[:, b : b + 1]
+            )
+
+        whs = []
+        for b in range(BLOCKS):
             wh = work.tile([P, NG * K], BF16, name="wh")
             nc.vector.tensor_tensor(
                 wh[:].rearrange("c (a e r) -> c a e r", a=NG, e=E),
-                feats[b][:].rearrange("c (a e r) -> c a e r", a=NG, e=E),
-                p[:].unsqueeze(1).unsqueeze(3).to_broadcast([P, NG, E, R]),
+                hb[:, b, :].rearrange("c (a e r) -> c a e r", a=NG, e=E),
+                p[:, b, :].unsqueeze(1).unsqueeze(3).to_broadcast([P, NG, E, R]),
                 MULT,
             )
-            half = work.tile([P, 1], F32, name="half")
-            nc.vector.tensor_scalar_mul(half[:], psumrow[:], 0.5)
-            q = work.tile([P, 1], F32, name="q")
-            nc.vector.reciprocal(q[:], half[:])
+            whs.append(wh)
+
+        half = held.tile([P, BLOCKS], F32, name="half")
+        nc.vector.tensor_scalar_mul(half[:], total[:], 0.5)
+        q = held.tile([P, BLOCKS], F32, name="q")
+        nc.vector.reciprocal(q[:], half[:])
+        q_spreads = []
+        for b in range(BLOCKS):
             q_spread = work.tile([P, N], F32, name="q_spread")
-            nc.gpsimd.tensor_copy(q_spread[:], q[:].to_broadcast([P, N]))
+            nc.gpsimd.tensor_copy(q_spread[:], q[:, b : b + 1].to_broadcast([P, N]))
+            q_spreads.append(q_spread)
+
+        flippeds = []
+        for b in range(BLOCKS):
             flipped_ps = psum.tile([K, NG * P], BF16, name="flipped_ps")
             for a in range(NG):
-                nc.tensor.transpose(flipped_ps[:, a * P : (a + 1) * P], wh[:, a * K : (a + 1) * K], identity[:])
+                nc.tensor.transpose(flipped_ps[:, a * P : (a + 1) * P], whs[b][:, a * K : (a + 1) * K], identity[:])
             flipped = work.tile([K, NG * P], BF16, name="flipped")
             nc.scalar.activation(flipped[:], flipped_ps[:], COPY)
+            flippeds.append(flipped)
+
+        for b in range(BLOCKS):
+            rows = slice(b * P, (b + 1) * P)
             u = psum.tile([P, N], F32, name="u")
             for a in range(NG):
                 nc.tensor.matmul(
                     u[:, a * OD : (a + 1) * OD],
-                    flipped[:, a * P : (a + 1) * P],
+                    flippeds[b][:, a * P : (a + 1) * P],
                     weights[:, a * OD : (a + 1) * OD],
                     start=True,
                     stop=True,
                 )
             u_sb = work.tile([P, N], F32, name="u_sb")
             nc.scalar.activation(u_sb[:], u[:], COPY)
-            nc.vector.tensor_tensor(windows[b][:].indirect(offsets[:]), u_sb[:], q_spread[:], MULT)
+            nc.vector.tensor_tensor(windows[b][:].indirect(offsets[:]), u_sb[:], q_spreads[b][:], MULT)
             nc.sync.dma_start(out[rows, :], windows[b][:])

@@ -29,17 +29,16 @@ def tile_moelora_s_kernel(tc, base, h, logits, bw, offs, out):
         lg = held.tile([P, BLOCKS, E], F32, name="lg")
         nc.sync.dma_start(lg[:], logits.rearrange("(b c) e -> c b e", c=P))
         hb = held.tile([P, BLOCKS, NG * K], F32, name="hb")
-        nc.scalar.dma_start(hb[:], h.rearrange("(b c) i -> c b i", c=P))
+        nc.sync.dma_start(hb[:], h.rearrange("(b c) i -> c b i", c=P))
+        weights = held.tile([K, N], BF16, name="weights")
+        nc.sync.dma_start(weights[:], bw)
         offsets = held.tile([P, N // 16], U16, name="offsets")
         nc.sync.dma_start(offsets[:], offs)
-        weights = held.tile([K, N], BF16, name="weights")
-        nc.scalar.dma_start(weights[:], bw)
         windows = []
         for b in range(BLOCKS):
             rows = slice(b * P, (b + 1) * P)
             window = work.tile([P, S], F32, name="window")
-            nc.sync.dma_start(window[:, : S // 2], base[rows, : S // 2])
-            nc.scalar.dma_start(window[:, S // 2 :], base[rows, S // 2 :])
+            nc.sync.dma_start(window[:], base[rows, :])
             windows.append(window)
 
         identity = held.tile([P, P], BF16, name="identity")

@@ -14,6 +14,7 @@ E, R, NG = 8, 16, 2
 K = E * R
 OD = N // NG
 BLOCKS = C // P
+WARM_MATMULS = 5
 
 FLOPS = 2 * C * N * K
 BYTES = 4 * C * (S - N) + 4 * C * NG * K + 4 * C * E + 2 * K * N + 2 * P * (N // 16) + 4 * C * S
@@ -23,8 +24,10 @@ def tile_moelora_s_kernel(tc, base, h, logits, bw, offs, out):
     nc = tc.nc
     with (
         tc.tile_pool(name="held", bufs=1) as held,
-        tc.tile_pool(name="work", bufs=BLOCKS) as work,
-        tc.psum_pool(name="psum", bufs=BLOCKS) as psum,
+        tc.tile_pool(name="wins", bufs=BLOCKS) as wins,
+        tc.tile_pool(name="work", bufs=BLOCKS * NG) as work,
+        tc.psum_pool(name="psum", bufs=2) as psum,
+        tc.psum_pool(name="idle", bufs=1) as idle,
     ):
         lg = held.tile([P, BLOCKS, E], F32, name="lg")
         nc.sync.dma_start(lg[:], logits.rearrange("(b c) e -> c b e", c=P))
@@ -37,7 +40,7 @@ def tile_moelora_s_kernel(tc, base, h, logits, bw, offs, out):
         windows = []
         for b in range(BLOCKS):
             rows = slice(b * P, (b + 1) * P)
-            window = work.tile([P, S], F32, name="window")
+            window = wins.tile([P, S], F32, name="window")
             nc.sync.dma_start(window[:], base[rows, :])
             windows.append(window)
 
@@ -48,6 +51,12 @@ def tile_moelora_s_kernel(tc, base, h, logits, bw, offs, out):
         warmed = held.tile([P, 1], F32, name="warmed")
         nc.scalar.activation(warmed[:], scratch[:], EXP)
 
+        zeros = held.tile([P, N], BF16, name="zeros")
+        nc.vector.memset(zeros[:], 0.0)
+        unread = idle.tile([P, N], F32, name="unread")
+        for i in range(WARM_MATMULS):
+            nc.tensor.matmul(unread[:], zeros[:, :P], zeros[:], start=True, stop=True)
+
         negmax = held.tile([P, BLOCKS], F32, name="negmax")
         nc.vector.tensor_reduce(negmax[:], lg[:], X, MAX, negate=True)
         p = held.tile([P, BLOCKS, E], F32, name="p")
@@ -57,16 +66,18 @@ def tile_moelora_s_kernel(tc, base, h, logits, bw, offs, out):
                 p[:, b, :], lg[:, b, :], EXP, bias=negmax[:, b : b + 1], scale=1.0, accum_out=total[:, b : b + 1]
             )
 
-        whs = []
-        for b in range(BLOCKS):
-            wh = work.tile([P, NG * K], BF16, name="wh")
+        units = [(b, a) for b in range(BLOCKS) for a in range(NG)]
+
+        whs = {}
+        for b, a in units:
+            wh = work.tile([P, K], BF16, name="wh")
             nc.vector.tensor_tensor(
-                wh[:].rearrange("c (a e r) -> c a e r", a=NG, e=E),
-                hb[:, b, :].rearrange("c (a e r) -> c a e r", a=NG, e=E),
-                p[:, b, :].unsqueeze(1).unsqueeze(3).to_broadcast([P, NG, E, R]),
+                wh[:].rearrange("c (e r) -> c e r", e=E),
+                hb[:, b, a * K : (a + 1) * K].rearrange("c (e r) -> c e r", e=E),
+                p[:, b, :].unsqueeze(2).to_broadcast([P, E, R]),
                 MULT,
             )
-            whs.append(wh)
+            whs[b, a] = wh
 
         half = held.tile([P, BLOCKS], F32, name="half")
         nc.vector.tensor_scalar_mul(half[:], total[:], 0.5)
@@ -74,31 +85,27 @@ def tile_moelora_s_kernel(tc, base, h, logits, bw, offs, out):
         nc.vector.reciprocal(q[:], half[:])
         q_spreads = []
         for b in range(BLOCKS):
-            q_spread = work.tile([P, N], F32, name="q_spread")
+            q_spread = held.tile([P, N], F32, name=f"q_spread{b}")
             nc.gpsimd.tensor_copy(q_spread[:], q[:, b : b + 1].to_broadcast([P, N]))
             q_spreads.append(q_spread)
 
-        flippeds = []
-        for b in range(BLOCKS):
-            flipped_ps = psum.tile([K, NG * P], BF16, name="flipped_ps")
-            for a in range(NG):
-                nc.tensor.transpose(flipped_ps[:, a * P : (a + 1) * P], whs[b][:, a * K : (a + 1) * K], identity[:])
-            flipped = work.tile([K, NG * P], BF16, name="flipped")
+        flippeds = {}
+        for b, a in units:
+            flipped_ps = psum.tile([K, P], BF16, name="flipped_ps")
+            nc.tensor.transpose(flipped_ps[:], whs[b, a][:], identity[:])
+            flipped = work.tile([K, P], BF16, name="flipped")
             nc.scalar.activation(flipped[:], flipped_ps[:], COPY)
-            flippeds.append(flipped)
+            flippeds[b, a] = flipped
+
+        u_sbs = [held.tile([P, N], F32, name=f"u_sb{b}") for b in range(BLOCKS)]
+        for b, a in units:
+            u = psum.tile([P, OD], F32, name="u")
+            nc.tensor.matmul(u[:], flippeds[b, a][:], weights[:, a * OD : (a + 1) * OD], start=True, stop=True)
+            if b == 0:
+                nc.vector.tensor_copy(u_sbs[b][:, a * OD : (a + 1) * OD], u[:])
+            else:
+                nc.scalar.activation(u_sbs[b][:, a * OD : (a + 1) * OD], u[:], COPY)
 
         for b in range(BLOCKS):
-            rows = slice(b * P, (b + 1) * P)
-            u = psum.tile([P, N], F32, name="u")
-            for a in range(NG):
-                nc.tensor.matmul(
-                    u[:, a * OD : (a + 1) * OD],
-                    flippeds[b][:, a * P : (a + 1) * P],
-                    weights[:, a * OD : (a + 1) * OD],
-                    start=True,
-                    stop=True,
-                )
-            u_sb = work.tile([P, N], F32, name="u_sb")
-            nc.scalar.activation(u_sb[:], u[:], COPY)
-            nc.vector.tensor_tensor(windows[b][:].indirect(offsets[:]), u_sb[:], q_spreads[b][:], MULT)
-            nc.sync.dma_start(out[rows, :], windows[b][:])
+            nc.vector.tensor_tensor(windows[b][:].indirect(offsets[:]), u_sbs[b][:], q_spreads[b][:], MULT)
+            nc.sync.dma_start(out[b * P : (b + 1) * P, :], windows[b][:])

@@ -14,7 +14,6 @@ E, R, NG = 8, 16, 2
 K = E * R
 OD = N // NG
 BLOCKS = C // P
-WARM_MATMULS = 5
 
 FLOPS = 2 * C * N * K
 BYTES = 4 * C * (S - N) + 4 * C * NG * K + 4 * C * E + 2 * K * N + 2 * P * (N // 16) + 4 * C * S
@@ -27,7 +26,6 @@ def tile_moelora_s_kernel(tc, base, h, logits, bw, offs, out):
         tc.tile_pool(name="wins", bufs=BLOCKS) as wins,
         tc.tile_pool(name="work", bufs=BLOCKS * NG) as work,
         tc.psum_pool(name="psum", bufs=2) as psum,
-        tc.psum_pool(name="idle", bufs=1) as idle,
     ):
         lg = held.tile([P, BLOCKS, E], F32, name="lg")
         nc.sync.dma_start(lg[:], logits.rearrange("(b c) e -> c b e", c=P))
@@ -50,12 +48,6 @@ def tile_moelora_s_kernel(tc, base, h, logits, bw, offs, out):
         nc.vector.memset(scratch[:], 0.0)
         warmed = held.tile([P, 1], F32, name="warmed")
         nc.scalar.activation(warmed[:], scratch[:], EXP)
-
-        zeros = held.tile([P, N], BF16, name="zeros")
-        nc.vector.memset(zeros[:], 0.0)
-        unread = idle.tile([P, N], F32, name="unread")
-        for i in range(WARM_MATMULS):
-            nc.tensor.matmul(unread[:], zeros[:, :P], zeros[:], start=True, stop=True)
 
         negmax = held.tile([P, BLOCKS], F32, name="negmax")
         nc.vector.tensor_reduce(negmax[:], lg[:], X, MAX, negate=True)

@@ -14,6 +14,8 @@ E, R, NG = 8, 16, 2
 K = E * R
 OD = N // NG
 BLOCKS = C // P
+SCALING = 2.0
+WARM_MATMULS = 5
 
 FLOPS = 2 * C * N * K
 BYTES = 4 * C * (S - N) + 4 * C * NG * K + 4 * C * E + 2 * K * N + 2 * P * (N // 16) + 4 * C * S
@@ -23,9 +25,9 @@ def tile_moelora_s_kernel(tc, base, h, logits, bw, offs, out):
     nc = tc.nc
     with (
         tc.tile_pool(name="held", bufs=1) as held,
-        tc.tile_pool(name="wins", bufs=BLOCKS) as wins,
-        tc.tile_pool(name="work", bufs=BLOCKS * NG) as work,
+        tc.tile_pool(name="work", bufs=BLOCKS) as work,
         tc.psum_pool(name="psum", bufs=2) as psum,
+        tc.psum_pool(name="idle", bufs=1) as idle,
     ):
         lg = held.tile([P, BLOCKS, E], F32, name="lg")
         nc.sync.dma_start(lg[:], logits.rearrange("(b c) e -> c b e", c=P))
@@ -38,7 +40,7 @@ def tile_moelora_s_kernel(tc, base, h, logits, bw, offs, out):
         windows = []
         for b in range(BLOCKS):
             rows = slice(b * P, (b + 1) * P)
-            window = wins.tile([P, S], F32, name="window")
+            window = work.tile([P, S], F32, name="window")
             nc.sync.dma_start(window[:], base[rows, :])
             windows.append(window)
 
@@ -49,54 +51,55 @@ def tile_moelora_s_kernel(tc, base, h, logits, bw, offs, out):
         warmed = held.tile([P, 1], F32, name="warmed")
         nc.scalar.activation(warmed[:], scratch[:], EXP)
 
+        zeros = held.tile([P, N], BF16, name="zeros")
+        nc.vector.memset(zeros[:], 0.0)
+        unread = idle.tile([P, N], F32, name="unread")
+        for i in range(WARM_MATMULS):
+            nc.tensor.matmul(unread[:], zeros[:, :P], zeros[:], start=True, stop=True)
+
         negmax = held.tile([P, BLOCKS], F32, name="negmax")
         nc.vector.tensor_reduce(negmax[:], lg[:], X, MAX, negate=True)
-        p = held.tile([P, BLOCKS, E], F32, name="p")
-        total = held.tile([P, BLOCKS], F32, name="total")
+        whs, q_spreads = [], []
         for b in range(BLOCKS):
-            nc.scalar.activation(
-                p[:, b, :], lg[:, b, :], EXP, bias=negmax[:, b : b + 1], scale=1.0, accum_out=total[:, b : b + 1]
-            )
-
-        units = [(b, a) for b in range(BLOCKS) for a in range(NG)]
-
-        whs = {}
-        for b, a in units:
-            wh = work.tile([P, K], BF16, name="wh")
-            nc.vector.tensor_tensor(
-                wh[:].rearrange("c (e r) -> c e r", e=E),
-                hb[:, b, a * K : (a + 1) * K].rearrange("c (e r) -> c e r", e=E),
-                p[:, b, :].unsqueeze(2).to_broadcast([P, E, R]),
-                MULT,
-            )
-            whs[b, a] = wh
-
-        half = held.tile([P, BLOCKS], F32, name="half")
-        nc.vector.tensor_scalar_mul(half[:], total[:], 0.5)
-        q = held.tile([P, BLOCKS], F32, name="q")
-        nc.vector.reciprocal(q[:], half[:])
-        q_spreads = []
-        for b in range(BLOCKS):
-            q_spread = held.tile([P, N], F32, name=f"q_spread{b}")
-            nc.gpsimd.tensor_copy(q_spread[:], q[:, b : b + 1].to_broadcast([P, N]))
+            p = work.tile([P, E], F32, name="p")
+            total = work.tile([P, 1], F32, name="total")
+            nc.scalar.activation(p[:], lg[:, b, :], EXP, bias=negmax[:, b : b + 1], scale=1.0, accum_out=total[:])
+            wh = [work.tile([P, K], BF16, name=f"wh{a}") for a in range(NG)]
+            for a in range(NG):
+                nc.vector.tensor_tensor(
+                    wh[a][:].rearrange("c (e r) -> c e r", e=E),
+                    hb[:, b, a * K : (a + 1) * K].rearrange("c (e r) -> c e r", e=E),
+                    p[:].unsqueeze(2).to_broadcast([P, E, R]),
+                    MULT,
+                )
+            whs.append(wh)
+            inverse = work.tile([P, 1], F32, name="inverse")
+            nc.vector.reciprocal(inverse[:], total[:])
+            q_spread = work.tile([P, N], F32, name="q_spread")
+            nc.scalar.activation(q_spread[:], inverse[:].to_broadcast([P, N]), COPY, scale=SCALING)
             q_spreads.append(q_spread)
 
-        flippeds = {}
-        for b, a in units:
-            flipped_ps = psum.tile([K, P], BF16, name="flipped_ps")
-            nc.tensor.transpose(flipped_ps[:], whs[b, a][:], identity[:])
-            flipped = work.tile([K, P], BF16, name="flipped")
-            nc.scalar.activation(flipped[:], flipped_ps[:], COPY)
-            flippeds[b, a] = flipped
-
-        u_sbs = [held.tile([P, N], F32, name=f"u_sb{b}") for b in range(BLOCKS)]
-        for b, a in units:
-            u = psum.tile([P, OD], F32, name="u")
-            nc.tensor.matmul(u[:], flippeds[b, a][:], weights[:, a * OD : (a + 1) * OD], start=True, stop=True)
-            if b == 0:
-                nc.vector.tensor_copy(u_sbs[b][:, a * OD : (a + 1) * OD], u[:])
-            else:
-                nc.scalar.activation(u_sbs[b][:, a * OD : (a + 1) * OD], u[:], COPY)
+        u_sbs = []
+        for b in range(BLOCKS):
+            flippeds = []
+            for a in range(NG):
+                flipped_ps = psum.tile([K, P], BF16, name="flipped_ps")
+                nc.tensor.transpose(flipped_ps[:], whs[b][a][:], identity[:])
+                flipped = work.tile([K, P], BF16, name=f"flipped{a}")
+                if b == 0:
+                    nc.vector.tensor_copy(flipped[:], flipped_ps[:])
+                else:
+                    nc.scalar.activation(flipped[:], flipped_ps[:], COPY)
+                flippeds.append(flipped)
+            u_sb = work.tile([P, N], F32, name="u_sb")
+            for a in range(NG):
+                u = psum.tile([P, OD], F32, name="u")
+                nc.tensor.matmul(u[:], flippeds[a][:], weights[:, a * OD : (a + 1) * OD], start=True, stop=True)
+                if b == 0:
+                    nc.vector.tensor_copy(u_sb[:, a * OD : (a + 1) * OD], u[:])
+                else:
+                    nc.scalar.activation(u_sb[:, a * OD : (a + 1) * OD], u[:], COPY)
+            u_sbs.append(u_sb)
 
         for b in range(BLOCKS):
             nc.vector.tensor_tensor(windows[b][:].indirect(offsets[:]), u_sbs[b][:], q_spreads[b][:], MULT)

@@ -15,7 +15,7 @@ K = E * R
 OD = N // NG
 BLOCKS = C // P
 SCALING = 2.0
-WARM_MATMULS = 5
+WARM_MATMULS = 4
 
 FLOPS = 2 * C * N * K
 BYTES = 4 * C * (S - N) + 4 * C * NG * K + 4 * C * E + 2 * K * N + 2 * P * (N // 16) + 4 * C * S

@@ -32,9 +32,9 @@ def tile_moelora_s_kernel(tc, base, h, logits, bw, offs, out):
         lg = held.tile([P, BLOCKS, E], F32, name="lg")
         nc.sync.dma_start(lg[:], logits.rearrange("(b c) e -> c b e", c=P))
         hb = held.tile([P, BLOCKS, NG * K], F32, name="hb")
-        nc.sync.dma_start(hb[:], h.rearrange("(b c) i -> c b i", c=P))
+        nc.scalar.dma_start(hb[:], h.rearrange("(b c) i -> c b i", c=P))
         weights = held.tile([K, N], BF16, name="weights")
-        nc.sync.dma_start(weights[:], bw)
+        nc.scalar.dma_start(weights[:], bw)
         offsets = held.tile([P, N // 16], U16, name="offsets")
         nc.sync.dma_start(offsets[:], offs)
         windows = []

@@ -31,18 +31,16 @@ def tile_moelora_s_kernel(tc, base, h, logits, bw, offs, out):
     ):
         lg = held.tile([P, BLOCKS, E], F32, name="lg")
         nc.sync.dma_start(lg[:], logits.rearrange("(b c) e -> c b e", c=P))
-        hb = held.tile([P, BLOCKS, NG * K], F32, name="hb")
-        nc.scalar.dma_start(hb[:], h.rearrange("(b c) i -> c b i", c=P))
+        hs = [work.tile([P, NG * K], F32, name="h_block") for b in range(BLOCKS)]
+        nc.scalar.dma_start(hs[0][:], h[0:P, :])
         weights = held.tile([K, N], BF16, name="weights")
         nc.scalar.dma_start(weights[:], bw)
         offsets = held.tile([P, N // 16], U16, name="offsets")
         nc.sync.dma_start(offsets[:], offs)
-        windows = []
-        for b in range(BLOCKS):
-            rows = slice(b * P, (b + 1) * P)
-            window = work.tile([P, S], F32, name="window")
-            nc.sync.dma_start(window[:], base[rows, :])
-            windows.append(window)
+        windows = [work.tile([P, S], F32, name="window") for b in range(BLOCKS)]
+        nc.sync.dma_start(windows[0][:], base[0:P, :])
+        nc.sync.dma_start(hs[1][:], h[P:C, :])
+        nc.sync.dma_start(windows[1][:], base[P:C, :])
 
         identity = held.tile([P, P], BF16, name="identity")
         make_identity(nc, identity[:])
@@ -59,32 +57,37 @@ def tile_moelora_s_kernel(tc, base, h, logits, bw, offs, out):
 
         negmax = held.tile([P, BLOCKS], F32, name="negmax")
         nc.vector.tensor_reduce(negmax[:], lg[:], X, MAX, negate=True)
-        whs, q_spreads = [], []
+        ps, q_spreads = [], []
         for b in range(BLOCKS):
             p = work.tile([P, E], F32, name="p")
             total = work.tile([P, 1], F32, name="total")
             nc.scalar.activation(p[:], lg[:, b, :], EXP, bias=negmax[:, b : b + 1], scale=1.0, accum_out=total[:])
-            wh = [work.tile([P, K], BF16, name=f"wh{a}") for a in range(NG)]
-            for a in range(NG):
-                nc.vector.tensor_tensor(
-                    wh[a][:].rearrange("c (e r) -> c e r", e=E),
-                    hb[:, b, a * K : (a + 1) * K].rearrange("c (e r) -> c e r", e=E),
-                    p[:].unsqueeze(2).to_broadcast([P, E, R]),
-                    MULT,
-                )
-            whs.append(wh)
+            ps.append(p)
             inverse = work.tile([P, 1], F32, name="inverse")
             nc.vector.reciprocal(inverse[:], total[:])
             q_spread = work.tile([P, N], F32, name="q_spread")
             nc.scalar.activation(q_spread[:], inverse[:].to_broadcast([P, N]), COPY, scale=SCALING)
             q_spreads.append(q_spread)
 
+        whs = [work.tile([P, NG * K], BF16, name="wh") for b in range(BLOCKS)]
+        for a in range(NG):
+            nc.vector.tensor_tensor(
+                whs[0][:, a * K : (a + 1) * K].rearrange("c (e r) -> c e r", e=E),
+                hs[0][:, a * K : (a + 1) * K].rearrange("c (e r) -> c e r", e=E),
+                ps[0][:].unsqueeze(2).to_broadcast([P, E, R]),
+                MULT,
+            )
+        wh_by_expert = whs[1][:].rearrange("c (a e r) -> c a e r", a=NG, e=E)
+        h_by_expert = hs[1][:].rearrange("c (a e r) -> c a e r", a=NG, e=E)
+        for e in range(E):
+            nc.scalar.activation(wh_by_expert[:, :, e, :], h_by_expert[:, :, e, :], COPY, scale=ps[1][:, e : e + 1])
+
         u_sbs = []
         for b in range(BLOCKS):
             flippeds = []
             for a in range(NG):
                 flipped_ps = psum.tile([K, P], BF16, name="flipped_ps")
-                nc.tensor.transpose(flipped_ps[:], whs[b][a][:], identity[:])
+                nc.tensor.transpose(flipped_ps[:], whs[b][:, a * K : (a + 1) * K], identity[:])
                 flipped = work.tile([K, P], BF16, name=f"flipped{a}")
                 if b == 0:
                     nc.vector.tensor_copy(flipped[:], flipped_ps[:])

@@ -40,20 +40,20 @@ def tile_moelora_s_kernel(tc, base, h, logits, bw, offs, out):
         windows = [work.tile([P, S], F32, name="window") for b in range(BLOCKS)]
         nc.sync.dma_start(windows[0][:], base[0:P, :])
         nc.sync.dma_start(hs[1][:], h[P:C, :])
-        nc.sync.dma_start(windows[1][:], base[P:C, :])
 
         identity = held.tile([P, P], BF16, name="identity")
         make_identity(nc, identity[:])
+        nc.gpsimd.dma_start(windows[1][:], base[P:C, :])
         scratch = held.tile([P, 1], F32, name="scratch")
         nc.vector.memset(scratch[:], 0.0)
         warmed = held.tile([P, 1], F32, name="warmed")
         nc.scalar.activation(warmed[:], scratch[:], EXP)
 
-        zeros = held.tile([P, N], BF16, name="zeros")
+        zeros = held.tile([P, P], BF16, name="zeros")
         nc.vector.memset(zeros[:], 0.0)
         unread = idle.tile([P, N], F32, name="unread")
         for i in range(WARM_MATMULS):
-            nc.tensor.matmul(unread[:], zeros[:, :P], zeros[:], start=True, stop=True)
+            nc.tensor.matmul(unread[:], zeros[:], zeros[:, 0:1].to_broadcast([P, N]), start=True, stop=True)
 
         negmax = held.tile([P, BLOCKS], F32, name="negmax")
         nc.vector.tensor_reduce(negmax[:], lg[:], X, MAX, negate=True)

@@ -26,6 +26,7 @@ def tile_moelora_s_kernel(tc, base, h, logits, bw, offs, out):
     with (
         tc.tile_pool(name="held", bufs=1) as held,
         tc.tile_pool(name="work", bufs=BLOCKS) as work,
+        tc.tile_pool(name="wide", bufs=2) as wide,
         tc.psum_pool(name="psum", bufs=2) as psum,
         tc.psum_pool(name="idle", bufs=1) as idle,
     ):
@@ -37,23 +38,24 @@ def tile_moelora_s_kernel(tc, base, h, logits, bw, offs, out):
         nc.scalar.dma_start(weights[:], bw)
         offsets = held.tile([P, N // 16], U16, name="offsets")
         nc.sync.dma_start(offsets[:], offs)
-        windows = [work.tile([P, S], F32, name="window") for b in range(BLOCKS)]
+        zeros = wide.tile([P, P], BF16, name="zeros", tag="wide")
+        nc.vector.memset(zeros[:], 0.0)
+        windows = [wide.tile([P, S], F32, name="window0", tag="wide")]
         nc.sync.dma_start(windows[0][:], base[0:P, :])
         nc.sync.dma_start(hs[1][:], h[P:C, :])
 
         identity = held.tile([P, P], BF16, name="identity")
         make_identity(nc, identity[:])
-        nc.gpsimd.dma_start(windows[1][:], base[P:C, :])
         scratch = held.tile([P, 1], F32, name="scratch")
         nc.vector.memset(scratch[:], 0.0)
         warmed = held.tile([P, 1], F32, name="warmed")
         nc.scalar.activation(warmed[:], scratch[:], EXP)
 
-        zeros = held.tile([P, P], BF16, name="zeros")
-        nc.vector.memset(zeros[:], 0.0)
         unread = idle.tile([P, N], F32, name="unread")
         for i in range(WARM_MATMULS):
             nc.tensor.matmul(unread[:], zeros[:], zeros[:, 0:1].to_broadcast([P, N]), start=True, stop=True)
+        windows.append(wide.tile([P, S], F32, name="window1", tag="wide"))
+        nc.gpsimd.dma_start(windows[1][:], base[P:C, :])
 
         negmax = held.tile([P, BLOCKS], F32, name="negmax")
         nc.vector.tensor_reduce(negmax[:], lg[:], X, MAX, negate=True)

@@ -38,24 +38,24 @@ def tile_moelora_s_kernel(tc, base, h, logits, bw, offs, out):
         nc.scalar.dma_start(weights[:], bw)
         offsets = held.tile([P, N // 16], U16, name="offsets")
         nc.sync.dma_start(offsets[:], offs)
-        zeros = wide.tile([P, P], BF16, name="zeros", tag="wide")
-        nc.vector.memset(zeros[:], 0.0)
+        scratch = wide.tile([P, 1], F32, name="scratch", tag="wide")
+        nc.vector.memset(scratch[:], 0.0)
         windows = [wide.tile([P, S], F32, name="window0", tag="wide")]
         nc.sync.dma_start(windows[0][:], base[0:P, :])
         nc.sync.dma_start(hs[1][:], h[P:C, :])
 
         identity = held.tile([P, P], BF16, name="identity")
         make_identity(nc, identity[:])
-        scratch = held.tile([P, 1], F32, name="scratch")
-        nc.vector.memset(scratch[:], 0.0)
         warmed = held.tile([P, 1], F32, name="warmed")
         nc.scalar.activation(warmed[:], scratch[:], EXP)
+        windows.append(wide.tile([P, S], F32, name="window1", tag="wide"))
+        nc.gpsimd.dma_start(windows[1][:], base[P:C, :])
 
+        zeros = held.tile([P, P], BF16, name="zeros")
+        nc.vector.memset(zeros[:], 0.0)
         unread = idle.tile([P, N], F32, name="unread")
         for i in range(WARM_MATMULS):
             nc.tensor.matmul(unread[:], zeros[:], zeros[:, 0:1].to_broadcast([P, N]), start=True, stop=True)
-        windows.append(wide.tile([P, S], F32, name="window1", tag="wide"))
-        nc.gpsimd.dma_start(windows[1][:], base[P:C, :])
 
         negmax = held.tile([P, BLOCKS], F32, name="negmax")
         nc.vector.tensor_reduce(negmax[:], lg[:], X, MAX, negate=True)

@@ -27,6 +27,7 @@ def tile_moelora_s_kernel(tc, base, h, logits, bw, offs, out):
         tc.tile_pool(name="held", bufs=1) as held,
         tc.tile_pool(name="work", bufs=BLOCKS) as work,
         tc.tile_pool(name="wide", bufs=2) as wide,
+        tc.tile_pool(name="turn", bufs=1) as turn,
         tc.psum_pool(name="psum", bufs=2) as psum,
         tc.psum_pool(name="idle", bufs=1) as idle,
     ):
@@ -38,6 +39,8 @@ def tile_moelora_s_kernel(tc, base, h, logits, bw, offs, out):
         nc.scalar.dma_start(weights[:], bw)
         offsets = held.tile([P, N // 16], U16, name="offsets")
         nc.sync.dma_start(offsets[:], offs)
+        zeros = held.tile([P, P], BF16, name="zeros")
+        nc.vector.memset(zeros[:], 0.0)
         scratch = wide.tile([P, 1], F32, name="scratch", tag="wide")
         nc.vector.memset(scratch[:], 0.0)
         windows = [wide.tile([P, S], F32, name="window0", tag="wide")]
@@ -51,60 +54,67 @@ def tile_moelora_s_kernel(tc, base, h, logits, bw, offs, out):
         windows.append(wide.tile([P, S], F32, name="window1", tag="wide"))
         nc.gpsimd.dma_start(windows[1][:], base[P:C, :])
 
-        zeros = held.tile([P, P], BF16, name="zeros")
-        nc.vector.memset(zeros[:], 0.0)
         unread = idle.tile([P, N], F32, name="unread")
         for i in range(WARM_MATMULS):
             nc.tensor.matmul(unread[:], zeros[:], zeros[:, 0:1].to_broadcast([P, N]), start=True, stop=True)
 
         negmax = held.tile([P, BLOCKS], F32, name="negmax")
         nc.vector.tensor_reduce(negmax[:], lg[:], X, MAX, negate=True)
-        ps, q_spreads = [], []
+        ps, totals = [], []
         for b in range(BLOCKS):
             p = work.tile([P, E], F32, name="p")
             total = work.tile([P, 1], F32, name="total")
             nc.scalar.activation(p[:], lg[:, b, :], EXP, bias=negmax[:, b : b + 1], scale=1.0, accum_out=total[:])
             ps.append(p)
-            inverse = work.tile([P, 1], F32, name="inverse")
-            nc.vector.reciprocal(inverse[:], total[:])
-            q_spread = work.tile([P, N], F32, name="q_spread")
-            nc.scalar.activation(q_spread[:], inverse[:].to_broadcast([P, N]), COPY, scale=SCALING)
-            q_spreads.append(q_spread)
+            totals.append(total)
 
-        whs = [work.tile([P, NG * K], BF16, name="wh") for b in range(BLOCKS)]
+        wh0 = held.tile([P, NG * K], BF16, name="wh0")
         for a in range(NG):
             nc.vector.tensor_tensor(
-                whs[0][:, a * K : (a + 1) * K].rearrange("c (e r) -> c e r", e=E),
+                wh0[:, a * K : (a + 1) * K].rearrange("c (e r) -> c e r", e=E),
                 hs[0][:, a * K : (a + 1) * K].rearrange("c (e r) -> c e r", e=E),
                 ps[0][:].unsqueeze(2).to_broadcast([P, E, R]),
                 MULT,
             )
-        wh_by_expert = whs[1][:].rearrange("c (a e r) -> c a e r", a=NG, e=E)
+
+        q_spreads = []
+        for b in range(BLOCKS):
+            inverse = work.tile([P, 1], F32, name="inverse")
+            nc.vector.reciprocal(inverse[:], totals[b][:])
+            q_spread = work.tile([P, N], F32, name="q_spread")
+            nc.scalar.activation(q_spread[:], inverse[:].to_broadcast([P, N]), COPY, scale=SCALING)
+            q_spreads.append(q_spread)
+
+        u_sbs = [work.tile([P, N], F32, name="u_sb") for b in range(BLOCKS)]
+        flippeds = [held.tile([K, P], BF16, name="flipped00"), turn.tile([K, P], BF16, name="flipped01", tag="turn")]
+        for a in range(NG):
+            flipped_ps = psum.tile([K, P], BF16, name="flipped_ps")
+            nc.tensor.transpose(flipped_ps[:], wh0[:, a * K : (a + 1) * K], identity[:])
+            nc.vector.tensor_copy(flippeds[a][:], flipped_ps[:])
+        for a in range(NG):
+            columns = slice(a * OD, (a + 1) * OD)
+            u = psum.tile([P, OD], F32, name="u")
+            nc.tensor.matmul(u[:], flippeds[a][:], weights[:, columns], start=True, stop=True)
+            if a == 0:
+                nc.vector.tensor_copy(u_sbs[0][:, columns], u[:])
+            else:
+                nc.scalar.activation(u_sbs[0][:, columns], u[:], COPY)
+
+        wh1 = turn.tile([P, NG * K], BF16, name="wh1", tag="turn")
+        wh_by_expert = wh1[:].rearrange("c (a e r) -> c a e r", a=NG, e=E)
         h_by_expert = hs[1][:].rearrange("c (a e r) -> c a e r", a=NG, e=E)
         for e in range(E):
             nc.scalar.activation(wh_by_expert[:, :, e, :], h_by_expert[:, :, e, :], COPY, scale=ps[1][:, e : e + 1])
-
-        u_sbs = []
-        for b in range(BLOCKS):
-            flippeds = []
-            for a in range(NG):
-                flipped_ps = psum.tile([K, P], BF16, name="flipped_ps")
-                nc.tensor.transpose(flipped_ps[:], whs[b][:, a * K : (a + 1) * K], identity[:])
-                flipped = work.tile([K, P], BF16, name=f"flipped{a}")
-                if b == 0:
-                    nc.vector.tensor_copy(flipped[:], flipped_ps[:])
-                else:
-                    nc.scalar.activation(flipped[:], flipped_ps[:], COPY)
-                flippeds.append(flipped)
-            u_sb = work.tile([P, N], F32, name="u_sb")
-            for a in range(NG):
-                u = psum.tile([P, OD], F32, name="u")
-                nc.tensor.matmul(u[:], flippeds[a][:], weights[:, a * OD : (a + 1) * OD], start=True, stop=True)
-                if b == 0:
-                    nc.vector.tensor_copy(u_sb[:, a * OD : (a + 1) * OD], u[:])
-                else:
-                    nc.scalar.activation(u_sb[:, a * OD : (a + 1) * OD], u[:], COPY)
-            u_sbs.append(u_sb)
+        flippeds = [held.tile([K, P], BF16, name=f"flipped1{a}") for a in range(NG)]
+        for a in range(NG):
+            flipped_ps = psum.tile([K, P], BF16, name="flipped_ps")
+            nc.tensor.transpose(flipped_ps[:], wh1[:, a * K : (a + 1) * K], identity[:])
+            nc.scalar.activation(flippeds[a][:], flipped_ps[:], COPY)
+        for a in range(NG):
+            columns = slice(a * OD, (a + 1) * OD)
+            u = psum.tile([P, OD], F32, name="u")
+            nc.tensor.matmul(u[:], flippeds[a][:], weights[:, columns], start=True, stop=True)
+            nc.scalar.activation(u_sbs[1][:, columns], u[:], COPY)
 
         for b in range(BLOCKS):
             nc.vector.tensor_tensor(windows[b][:].indirect(offsets[:]), u_sbs[b][:], q_spreads[b][:], MULT)

import concourse.mybir as mybir
from concourse.masks import make_identity

F32, BF16, U16 = mybir.dt.float32, mybir.dt.bfloat16, mybir.dt.uint16
MULT = mybir.AluOpType.mult
MAX = mybir.AluOpType.max
EXP = mybir.ActivationFunctionType.Exp
COPY = mybir.ActivationFunctionType.Copy
X = mybir.AxisListType.X

P = 128
C, S, N = 256, 2048, 512
E, R, NG = 8, 16, 2
K = E * R
OD = N // NG
BLOCKS = C // P
SCALING = 2.0
WARM_MATMULS = 4

FLOPS = 2 * C * N * K
BYTES = 4 * C * (S - N) + 4 * C * NG * K + 4 * C * E + 2 * K * N + 2 * P * (N // 16) + 4 * C * S


def tile_moelora_s_kernel(tc, base, h, logits, bw, offs, out):
    nc = tc.nc
    with (
        tc.tile_pool(name="held", bufs=1) as held,
        tc.tile_pool(name="work", bufs=BLOCKS) as work,
        tc.tile_pool(name="wide", bufs=2) as wide,
        tc.tile_pool(name="turn", bufs=1) as turn,
        tc.psum_pool(name="psum", bufs=2) as psum,
        tc.psum_pool(name="idle", bufs=1) as idle,
    ):
        lg = held.tile([P, BLOCKS, E], F32, name="lg")
        nc.sync.dma_start(lg[:], logits.rearrange("(b c) e -> c b e", c=P))
        hs = [work.tile([P, NG * K], F32, name="h_block") for b in range(BLOCKS)]
        nc.scalar.dma_start(hs[0][:], h[0:P, :])
        weights = held.tile([K, N], BF16, name="weights")
        nc.scalar.dma_start(weights[:], bw)
        offsets = held.tile([P, N // 16], U16, name="offsets")
        nc.sync.dma_start(offsets[:], offs)
        zeros = held.tile([P, P], BF16, name="zeros")
        nc.vector.memset(zeros[:], 0.0)
        scratch = wide.tile([P, 1], F32, name="scratch", tag="wide")
        nc.vector.memset(scratch[:], 0.0)
        windows = [wide.tile([P, S], F32, name="window0", tag="wide")]
        nc.sync.dma_start(windows[0][:], base[0:P, :])
        nc.sync.dma_start(hs[1][:], h[P:C, :])

        identity = held.tile([P, P], BF16, name="identity")
        make_identity(nc, identity[:])
        warmed = held.tile([P, 1], F32, name="warmed")
        nc.scalar.activation(warmed[:], scratch[:], EXP)
        windows.append(wide.tile([P, S], F32, name="window1", tag="wide"))
        nc.gpsimd.dma_start(windows[1][:], base[P:C, :])

        unread = idle.tile([P, N], F32, name="unread")
        for i in range(WARM_MATMULS):
            nc.tensor.matmul(unread[:], zeros[:], zeros[:, 0:1].to_broadcast([P, N]), start=True, stop=True)

        negmax = held.tile([P, BLOCKS], F32, name="negmax")
        nc.vector.tensor_reduce(negmax[:], lg[:], X, MAX, negate=True)
        ps, totals = [], []
        for b in range(BLOCKS):
            p = work.tile([P, E], F32, name="p")
            total = work.tile([P, 1], F32, name="total")
            nc.scalar.activation(p[:], lg[:, b, :], EXP, bias=negmax[:, b : b + 1], scale=1.0, accum_out=total[:])
            ps.append(p)
            totals.append(total)

        wh0 = held.tile([P, NG * K], BF16, name="wh0")
        for a in range(NG):
            nc.vector.tensor_tensor(
                wh0[:, a * K : (a + 1) * K].rearrange("c (e r) -> c e r", e=E),
                hs[0][:, a * K : (a + 1) * K].rearrange("c (e r) -> c e r", e=E),
                ps[0][:].unsqueeze(2).to_broadcast([P, E, R]),
                MULT,
            )

        q_spreads = []
        for b in range(BLOCKS):
            inverse = work.tile([P, 1], F32, name="inverse")
            nc.vector.reciprocal(inverse[:], totals[b][:])
            q_spread = work.tile([P, N], F32, name="q_spread")
            nc.scalar.activation(q_spread[:], inverse[:].to_broadcast([P, N]), COPY, scale=SCALING)
            q_spreads.append(q_spread)

        u_sbs = [work.tile([P, N], F32, name="u_sb") for b in range(BLOCKS)]
        flippeds = [held.tile([K, P], BF16, name="flipped00"), turn.tile([K, P], BF16, name="flipped01", tag="turn")]
        for a in range(NG):
            flipped_ps = psum.tile([K, P], BF16, name="flipped_ps")
            nc.tensor.transpose(flipped_ps[:], wh0[:, a * K : (a + 1) * K], identity[:])
            nc.vector.tensor_copy(flippeds[a][:], flipped_ps[:])
        for a in range(NG):
            columns = slice(a * OD, (a + 1) * OD)
            u = psum.tile([P, OD], F32, name="u")
            nc.tensor.matmul(u[:], flippeds[a][:], weights[:, columns], start=True, stop=True)
            if a == 0:
                nc.vector.tensor_copy(u_sbs[0][:, columns], u[:])
            else:
                nc.scalar.activation(u_sbs[0][:, columns], u[:], COPY)

        wh1 = turn.tile([P, NG * K], BF16, name="wh1", tag="turn")
        wh_by_expert = wh1[:].rearrange("c (a e r) -> c a e r", a=NG, e=E)
        h_by_expert = hs[1][:].rearrange("c (a e r) -> c a e r", a=NG, e=E)
        for e in range(E):
            nc.scalar.activation(wh_by_expert[:, :, e, :], h_by_expert[:, :, e, :], COPY, scale=ps[1][:, e : e + 1])
        flippeds = [held.tile([K, P], BF16, name=f"flipped1{a}") for a in range(NG)]
        for a in range(NG):
            flipped_ps = psum.tile([K, P], BF16, name="flipped_ps")
            nc.tensor.transpose(flipped_ps[:], wh1[:, a * K : (a + 1) * K], identity[:])
            nc.scalar.activation(flippeds[a][:], flipped_ps[:], COPY)
        for a in range(NG):
            columns = slice(a * OD, (a + 1) * OD)
            u = psum.tile([P, OD], F32, name="u")
            nc.tensor.matmul(u[:], flippeds[a][:], weights[:, columns], start=True, stop=True)
            nc.scalar.activation(u_sbs[1][:, columns], u[:], COPY)

        for b in range(BLOCKS):
            nc.vector.tensor_tensor(windows[b][:].indirect(offsets[:]), u_sbs[b][:], q_spreads[b][:], MULT)
            nc.sync.dma_start(out[b * P : (b + 1) * P, :], windows[b][:])
